import numpy as np
import ml_dtypes


def mxq(x, axis, fmt="e4m3"):
    dtype, down = {"e4m3": (ml_dtypes.float8_e4m3fn, 7), "e5m2": (ml_dtypes.float8_e5m2, 14)}[fmt]
    v = np.moveaxis(np.asarray(x, np.float32).astype(ml_dtypes.bfloat16).astype(np.float64), axis, -1)
    blocks = v.reshape(v.shape[:-1] + (-1, 32))
    amax = np.abs(blocks).max(-1, keepdims=True)
    byte = np.maximum(np.where(amax > 0, np.frexp(amax)[1] - 1 + 127, 0) - down, 1)
    scale = np.exp2(byte - 127.0)
    codes = (blocks / scale).astype(np.float32).astype(dtype).astype(np.float64)
    return np.moveaxis((codes * scale).reshape(v.shape), -1, axis)


WIDE = False


def mx_kscale(k):
    if not WIDE:
        return np.ones(k)
    levels = np.array([10, -10, 5, -5, 0])
    a = np.random.permutation(np.resize(levels, k // 512 * 4)).reshape(k // 512, 4)
    idx = np.arange(k)
    return np.exp2(a[idx // 512, idx % 128 // 32])


BF16 = ml_dtypes.bfloat16


def bf(x):
    return np.asarray(x, np.float32).astype(BF16)


def f64(x):
    return np.asarray(x).astype(np.float64)


B, T, D, H, G, HD, W = 1, 8192, 512, 2, 1, 128, 256
EPS = 1e-6


def rmsnorm(u, w):
    var = np.mean(u * u, axis=-1, keepdims=True)
    return u * (1.0 / np.sqrt(var + EPS)) * (1.0 + w)


def setup_inputs():
    s = mx_kscale(D)
    return {"x": bf(np.random.standard_normal((B, T, D)) * s),
            "Wq": bf(np.random.standard_normal((D, H * HD)) * 0.005 / np.sqrt(D) / s[:, None]),
            "Wk": bf(np.random.standard_normal((D, G * HD)) * 0.005 / np.sqrt(D) / s[:, None]),
            "Wv": bf(np.random.standard_normal((D, G * HD)) * 1.0 / np.sqrt(D) / s[:, None]),
            "q_scale": bf(np.random.standard_normal(HD) * 0.2),
            "k_scale": bf(np.random.standard_normal(HD) * 0.2)}


def reference(x, Wq, Wk, Wv, q_scale, k_scale):
    xq = mxq(f64(x), 2, "e4m3")
    q = (xq @ mxq(f64(Wq), 0, "e4m3")).reshape(B, T, H, HD).transpose(0, 2, 1, 3)
    k = (xq @ mxq(f64(Wk), 0, "e4m3")).reshape(B, T, G, HD).transpose(0, 2, 1, 3)
    v = (xq @ mxq(f64(Wv), 0, "e4m3")).reshape(B, T, G, HD).transpose(0, 2, 1, 3)
    return rmsnorm(q, f64(q_scale)), rmsnorm(k, f64(k_scale)), v

@@ -1,0 +1,230 @@
+from contextlib import ExitStack
+
+import concourse.mybir as mybir
+from concourse.masks import make_identity
+
+F32 = mybir.dt.float32
+BF16 = mybir.dt.bfloat16
+U32 = mybir.dt.uint32
+U8 = mybir.dt.uint8
+FP8X4 = mybir.dt.float8_e4m3fn_x4
+ACT = mybir.ActivationFunctionType
+ALU = mybir.AluOpType
+
+P = 128
+TOKENS = 8192
+K = 512
+PACK = 4
+HD = 128
+HEADS = 4
+NORMED = 3
+N_OUT = HEADS * HD
+EPS = 1e-6
+
+TILES = TOKENS // P
+UNIT = 2
+UNITS = TILES // UNIT
+LOAD_TILES = 4
+STORE_TILES = 8
+WORDS = K // 2
+
+FLOPS = 2 * TOKENS * K * N_OUT
+
+
+def tile_groupedqueryattention_pa_t_kernel(
+    tc, x, Wq, Wk, Wv, q_scale, k_scale, out_0, out_1, out_2
+):
+    nc = tc.nc
+    with ExitStack() as ctx:
+        ctx.enter_context(tc.manual_schedule())
+        consts = ctx.enter_context(tc.tile_pool(name="consts", bufs=1))
+        xin = ctx.enter_context(tc.tile_pool(name="xin", bufs=TILES // LOAD_TILES))
+        work = ctx.enter_context(tc.tile_pool(name="work", bufs=3))
+        stages = ctx.enter_context(tc.tile_pool(name="stages", bufs=6))
+        psum_xt = ctx.enter_context(tc.psum_pool(name="psum_xt", bufs=2))
+        psum_acc = ctx.enter_context(tc.psum_pool(name="psum_acc", bufs=6))
+
+        w_raws = []
+        for w_dram, w_cols in ((Wq, 2 * HD), (Wk, HD), (Wv, HD)):
+            w_raw = consts.tile([P, PACK, w_cols], BF16, name="w_raw%d" % len(w_raws))
+            nc.sync.dma_start(
+                out=w_raw[:].rearrange("p (u e) c -> p u e c", u=2),
+                in_=w_dram.rearrange("(u p e) c -> p u e c", u=2, e=2),
+            )
+            w_raws.append(w_raw)
+
+        x_view = x.flatten_outer_dims().rearrange("(p j) k -> p j k", p=P)
+        x_words = []
+        for c in range(TILES // LOAD_TILES):
+            x_chunk = xin.tile([P, LOAD_TILES, K], BF16)
+            nc.sync.dma_start(
+                out=x_chunk[:], in_=x_view[:, c * LOAD_TILES : (c + 1) * LOAD_TILES, :]
+            )
+            x_words.append(x_chunk[:].rearrange("p j k -> p (j k)").bitcast(F32))
+
+        eps = consts.tile([P, 1], F32)
+        nc.vector.memset(eps[:], EPS)
+        ones = consts.tile([P, P], BF16)
+        nc.vector.memset(ones[:], 1.0)
+        gain_rows = consts.tile([P, 2 * HD], BF16)
+        nc.vector.memset(gain_rows[:], 0.0)
+        nc.scalar.dma_start(out=gain_rows[0:1, 0:HD], in_=q_scale.rearrange("(o d) -> o d", o=1))
+        nc.scalar.dma_start(
+            out=gain_rows[0:1, HD : 2 * HD], in_=k_scale.rearrange("(o d) -> o d", o=1)
+        )
+        warm = consts.tile([P, 1], F32)
+        nc.scalar.activation(out=warm[:], in_=eps[:], func=ACT.Abs_reciprocal_sqrt)
+        ident = consts.tile([P, P], F32)
+        make_identity(nc, ident[:])
+
+        w_grouped = consts.tile([P, N_OUT, PACK], BF16, align_bytes=64)
+        nc.vector.tensor_copy(
+            out=w_grouped[:, 0 : 2 * HD, :], in_=w_raws[0][:].rearrange("p t c -> p c t")
+        )
+        nc.scalar.copy(
+            out=w_grouped[:, 2 * HD : 3 * HD, :], in_=w_raws[1][:].rearrange("p t c -> p c t")
+        )
+        nc.scalar.copy(
+            out=w_grouped[:, 3 * HD : 4 * HD, :], in_=w_raws[2][:].rearrange("p t c -> p c t")
+        )
+        w_codes = consts.tile([P, N_OUT], U32, align_bytes=64)
+        w_scales = consts.tile([P, N_OUT], U8, align_bytes=64)
+        nc.vector.quantize_mx(
+            out=w_codes[:].bitcast(FP8X4),
+            scales=w_scales[:],
+            in_=w_grouped[:].rearrange("p c t -> p (c t)"),
+        )
+
+        gain_ps = psum_acc.tile([P, N_OUT], F32, tag="acc")
+        nc.tensor.matmul(
+            out=gain_ps[:, 0 : 2 * HD], lhsT=ones[:], rhs=gain_rows[:], start=True, stop=True
+        )
+        gain = consts.tile([P, 2 * HD], F32)
+        nc.vector.tensor_scalar_add(out=gain[:], in0=gain_ps[:, 0 : 2 * HD], scalar1=1.0)
+
+        out_views = [
+            out_0.flatten_outer_dims().rearrange("(h p j) d -> h p j d", h=2, p=P)[0],
+            out_0.flatten_outer_dims().rearrange("(h p j) d -> h p j d", h=2, p=P)[1],
+            out_1.flatten_outer_dims().rearrange("(p j) d -> p j d", p=P),
+            out_2.flatten_outer_dims().rearrange("(p j) d -> p j d", p=P),
+        ]
+
+        live = {}
+
+        def transposes(u):
+            xt = psum_xt.tile([P, UNIT, 2, P], F32)
+            for i in range(UNIT):
+                j = u * UNIT + i
+                words = x_words[j // LOAD_TILES]
+                first = (j % LOAD_TILES) * WORDS
+                for half in range(2):
+                    nc.tensor.transpose(
+                        xt[:, i, half, :],
+                        words[:, first + half * P : first + (half + 1) * P],
+                        ident[:],
+                    )
+            live["xt", u] = xt
+
+        def copy_out(u):
+            grouped = work.tile([P, UNIT * P * PACK], BF16, align_bytes=64)
+            nc.scalar.copy(
+                out=grouped[:].bitcast(F32).rearrange("p (i n h) -> p i n h", i=UNIT, h=2),
+                in_=live["xt", u][:].rearrange("p i h n -> p i n h"),
+            )
+            live["grouped", u] = grouped
+
+        def quantise(u):
+            codes = work.tile([P, UNIT * P], U32, align_bytes=64)
+            scales = work.tile([P, UNIT * P], U8, align_bytes=64)
+            nc.vector.quantize_mx(
+                out=codes[:].bitcast(FP8X4), scales=scales[:], in_=live["grouped", u][:]
+            )
+            live["codes", u] = (codes, scales)
+
+        def project(u):
+            codes, scales = live["codes", u]
+            accs = []
+            for i in range(UNIT):
+                acc = psum_acc.tile([P, N_OUT], F32, tag="acc")
+                nc.tensor.matmul_mx(
+                    out=acc[:],
+                    lhsT=codes[:, i * P : (i + 1) * P].bitcast(FP8X4),
+                    lhsT_scale=scales[:, i * P : (i + 1) * P],
+                    rhs=w_codes[:].bitcast(FP8X4),
+                    rhs_scale=w_scales[:],
+                    start=True,
+                    stop=True,
+                )
+                accs.append(acc)
+            live["accs", u] = accs
+
+        def squares(u):
+            squared = work.tile([P, UNIT * NORMED, HD], F32)
+            sums = work.tile([P, UNIT * NORMED], F32)
+            for i in range(UNIT):
+                for h in range(NORMED):
+                    c = i * NORMED + h
+                    nc.scalar.activation(
+                        out=squared[:, c, :],
+                        in_=live["accs", u][i][:, h * HD : (h + 1) * HD],
+                        func=ACT.Square,
+                        accum_out=sums[:, c : c + 1],
+                    )
+            live["sums", u] = sums
+
+        def inverse_rms(u):
+            rstd = work.tile([P, UNIT * NORMED], F32)
+            nc.scalar.activation(
+                out=rstd[:],
+                in_=live["sums", u][:],
+                func=ACT.Abs_reciprocal_sqrt,
+                scale=1.0 / HD,
+                bias=eps[:],
+            )
+            live["rstd", u] = rstd
+
+        def write_out(u):
+            first_tile = u * UNIT
+            if first_tile % STORE_TILES == 0:
+                stage = stages.tile([P, HEADS, STORE_TILES, HD], F32)
+                live["stage"] = stage
+            stage = live["stage"]
+            rstd = live["rstd", u]
+            accs = live["accs", u]
+            for i in range(UNIT):
+                s = (first_tile + i) % STORE_TILES
+                for h in range(NORMED):
+                    c = i * NORMED + h
+                    g = h // 2
+                    nc.vector.scalar_tensor_tensor(
+                        out=stage[:, h, s, :],
+                        in0=accs[i][:, h * HD : (h + 1) * HD],
+                        scalar=rstd[:, c : c + 1],
+                        in1=gain[:, g * HD : (g + 1) * HD],
+                        op0=ALU.mult,
+                        op1=ALU.mult,
+                    )
+                nc.vector.tensor_copy(
+                    out=stage[:, NORMED, s, :], in_=accs[i][:, NORMED * HD : N_OUT]
+                )
+            if (first_tile + UNIT) % STORE_TILES == 0:
+                j0 = first_tile + UNIT - STORE_TILES
+                for h in range(HEADS):
+                    nc.sync.dma_start(
+                        out=out_views[h][:, j0 : j0 + STORE_TILES, :], in_=stage[:, h, :, :]
+                    )
+
+        for r in range(-2, UNITS + 1):
+            if 0 <= r + 2 < UNITS:
+                transposes(r + 2)
+            if 0 <= r + 1 < UNITS:
+                quantise(r + 1)
+                project(r + 1)
+            if 0 <= r < UNITS:
+                squares(r)
+            if 0 <= r + 2 < UNITS:
+                copy_out(r + 2)
+            if 0 <= r < UNITS:
+                inverse_rms(r)
+            if 0 <= r - 1 < UNITS:
+                write_out(r - 1)

@@ -24,9 +24,9 @@ EPS = 1e-6
 TILES = TOKENS // P
 UNIT = 2
 UNITS = TILES // UNIT
-LOAD_TILES = 4
+LOAD_TILES = 8
 STORE_TILES = 8
-WORDS = K // 2
+VECTOR_COPY_EVERY = 4
 
 FLOPS = 2 * TOKENS * K * N_OUT
 
@@ -38,7 +38,7 @@ def tile_groupedqueryattention_pa_t_kernel(
     with ExitStack() as ctx:
         ctx.enter_context(tc.manual_schedule())
         consts = ctx.enter_context(tc.tile_pool(name="consts", bufs=1))
-        xin = ctx.enter_context(tc.tile_pool(name="xin", bufs=TILES // LOAD_TILES))
+        xin = ctx.enter_context(tc.tile_pool(name="xin", bufs=1))
         work = ctx.enter_context(tc.tile_pool(name="work", bufs=3))
         stages = ctx.enter_context(tc.tile_pool(name="stages", bufs=6))
         psum_xt = ctx.enter_context(tc.psum_pool(name="psum_xt", bufs=2))
@@ -54,13 +54,14 @@ def tile_groupedqueryattention_pa_t_kernel(
             w_raws.append(w_raw)
 
         x_view = x.flatten_outer_dims().rearrange("(p j) k -> p j k", p=P)
+        load_sizes = [UNIT] * (LOAD_TILES // UNIT) + [LOAD_TILES] * (TILES // LOAD_TILES - 1)
         x_words = []
-        for c in range(TILES // LOAD_TILES):
-            x_chunk = xin.tile([P, LOAD_TILES, K], BF16)
-            nc.sync.dma_start(
-                out=x_chunk[:], in_=x_view[:, c * LOAD_TILES : (c + 1) * LOAD_TILES, :]
-            )
-            x_words.append(x_chunk[:].rearrange("p j k -> p (j k)").bitcast(F32))
+        for size in load_sizes:
+            j0 = len(x_words)
+            x_chunk = xin.tile([P, size, K], BF16, name="x_chunk%d" % j0)
+            nc.sync.dma_start(out=x_chunk[:], in_=x_view[:, j0 : j0 + size, :])
+            for j in range(size):
+                x_words.append(x_chunk[:, j, :].bitcast(F32))
 
         eps = consts.tile([P, 1], F32)
         nc.vector.memset(eps[:], EPS)
@@ -95,12 +96,14 @@ def tile_groupedqueryattention_pa_t_kernel(
             in_=w_grouped[:].rearrange("p c t -> p (c t)"),
         )
 
-        gain_ps = psum_acc.tile([P, N_OUT], F32, tag="acc")
-        nc.tensor.matmul(
-            out=gain_ps[:, 0 : 2 * HD], lhsT=ones[:], rhs=gain_rows[:], start=True, stop=True
-        )
         gain = consts.tile([P, 2 * HD], F32)
-        nc.vector.tensor_scalar_add(out=gain[:], in0=gain_ps[:, 0 : 2 * HD], scalar1=1.0)
+
+        def spread_gains():
+            gain_ps = psum_acc.tile([P, N_OUT], F32, tag="acc")
+            nc.tensor.matmul(
+                out=gain_ps[:, 0 : 2 * HD], lhsT=ones[:], rhs=gain_rows[:], start=True, stop=True
+            )
+            nc.vector.tensor_scalar_add(out=gain[:], in0=gain_ps[:, 0 : 2 * HD], scalar1=1.0)
 
         out_views = [
             out_0.flatten_outer_dims().rearrange("(h p j) d -> h p j d", h=2, p=P)[0],
@@ -114,23 +117,22 @@ def tile_groupedqueryattention_pa_t_kernel(
         def transposes(u):
             xt = psum_xt.tile([P, UNIT, 2, P], F32)
             for i in range(UNIT):
-                j = u * UNIT + i
-                words = x_words[j // LOAD_TILES]
-                first = (j % LOAD_TILES) * WORDS
                 for half in range(2):
                     nc.tensor.transpose(
                         xt[:, i, half, :],
-                        words[:, first + half * P : first + (half + 1) * P],
+                        x_words[u * UNIT + i][:, half * P : (half + 1) * P],
                         ident[:],
                     )
             live["xt", u] = xt
 
         def copy_out(u):
             grouped = work.tile([P, UNIT * P * PACK], BF16, align_bytes=64)
-            nc.scalar.copy(
-                out=grouped[:].bitcast(F32).rearrange("p (i n h) -> p i n h", i=UNIT, h=2),
-                in_=live["xt", u][:].rearrange("p i h n -> p i n h"),
-            )
+            interleaved = grouped[:].bitcast(F32).rearrange("p (i n h) -> p i n h", i=UNIT, h=2)
+            planes = live["xt", u][:].rearrange("p i h n -> p i n h")
+            if u % VECTOR_COPY_EVERY == VECTOR_COPY_EVERY - 1:
+                nc.vector.tensor_copy(out=interleaved, in_=planes)
+            else:
+                nc.scalar.copy(out=interleaved, in_=planes)
             live["grouped", u] = grouped
 
         def quantise(u):
@@ -207,14 +209,23 @@ def tile_groupedqueryattention_pa_t_kernel(
                 nc.vector.tensor_copy(
                     out=stage[:, NORMED, s, :], in_=accs[i][:, NORMED * HD : N_OUT]
                 )
-            if (first_tile + UNIT) % STORE_TILES == 0:
-                j0 = first_tile + UNIT - STORE_TILES
+            if first_tile >= TILES - STORE_TILES:
+                stored = UNIT
+            elif (first_tile + UNIT) % STORE_TILES == 0:
+                stored = STORE_TILES
+            else:
+                stored = 0
+            if stored > 0:
+                j0 = first_tile + UNIT - stored
+                s0 = j0 % STORE_TILES
                 for h in range(HEADS):
                     nc.sync.dma_start(
-                        out=out_views[h][:, j0 : j0 + STORE_TILES, :], in_=stage[:, h, :, :]
+                        out=out_views[h][:, j0 : j0 + stored, :], in_=stage[:, h, s0 : s0 + stored, :]
                     )
 
         for r in range(-2, UNITS + 1):
+            if r == 0:
+                spread_gains()
             if 0 <= r + 2 < UNITS:
                 transposes(r + 2)
             if 0 <= r + 1 < UNITS:

@@ -26,7 +26,6 @@ UNIT = 2
 UNITS = TILES // UNIT
 LOAD_TILES = 8
 STORE_TILES = 8
-VECTOR_COPY_EVERY = 4
 
 FLOPS = 2 * TOKENS * K * N_OUT
 
@@ -129,10 +128,7 @@ def tile_groupedqueryattention_pa_t_kernel(
             grouped = work.tile([P, UNIT * P * PACK], BF16, align_bytes=64)
             interleaved = grouped[:].bitcast(F32).rearrange("p (i n h) -> p i n h", i=UNIT, h=2)
             planes = live["xt", u][:].rearrange("p i h n -> p i n h")
-            if u % VECTOR_COPY_EVERY == VECTOR_COPY_EVERY - 1:
-                nc.vector.tensor_copy(out=interleaved, in_=planes)
-            else:
-                nc.scalar.copy(out=interleaved, in_=planes)
+            nc.scalar.copy(out=interleaved, in_=planes)
             live["grouped", u] = grouped
 
         def quantise(u):

from contextlib import ExitStack

import concourse.mybir as mybir
from concourse.masks import make_identity

F32 = mybir.dt.float32
BF16 = mybir.dt.bfloat16
U32 = mybir.dt.uint32
U8 = mybir.dt.uint8
FP8X4 = mybir.dt.float8_e4m3fn_x4
ACT = mybir.ActivationFunctionType
ALU = mybir.AluOpType

P = 128
TOKENS = 8192
K = 512
PACK = 4
HD = 128
HEADS = 4
NORMED = 3
N_OUT = HEADS * HD
EPS = 1e-6

TILES = TOKENS // P
UNIT = 2
UNITS = TILES // UNIT
LOAD_TILES = 8
STORE_TILES = 8

FLOPS = 2 * TOKENS * K * N_OUT


def tile_groupedqueryattention_pa_t_kernel(
    tc, x, Wq, Wk, Wv, q_scale, k_scale, out_0, out_1, out_2
):
    nc = tc.nc
    with ExitStack() as ctx:
        ctx.enter_context(tc.manual_schedule())
        consts = ctx.enter_context(tc.tile_pool(name="consts", bufs=1))
        xin = ctx.enter_context(tc.tile_pool(name="xin", bufs=1))
        work = ctx.enter_context(tc.tile_pool(name="work", bufs=3))
        stages = ctx.enter_context(tc.tile_pool(name="stages", bufs=6))
        psum_xt = ctx.enter_context(tc.psum_pool(name="psum_xt", bufs=2))
        psum_acc = ctx.enter_context(tc.psum_pool(name="psum_acc", bufs=6))

        w_raws = []
        for w_dram, w_cols in ((Wq, 2 * HD), (Wk, HD), (Wv, HD)):
            w_raw = consts.tile([P, PACK, w_cols], BF16, name="w_raw%d" % len(w_raws))
            nc.sync.dma_start(
                out=w_raw[:].rearrange("p (u e) c -> p u e c", u=2),
                in_=w_dram.rearrange("(u p e) c -> p u e c", u=2, e=2),
            )
            w_raws.append(w_raw)

        x_view = x.flatten_outer_dims().rearrange("(p j) k -> p j k", p=P)
        load_sizes = [UNIT] * (LOAD_TILES // UNIT) + [LOAD_TILES] * (TILES // LOAD_TILES - 1)
        x_words = []
        for size in load_sizes:
            j0 = len(x_words)
            x_chunk = xin.tile([P, size, K], BF16, name="x_chunk%d" % j0)
            nc.sync.dma_start(out=x_chunk[:], in_=x_view[:, j0 : j0 + size, :])
            for j in range(size):
                x_words.append(x_chunk[:, j, :].bitcast(F32))

        eps = consts.tile([P, 1], F32)
        nc.vector.memset(eps[:], EPS)
        ones = consts.tile([P, P], BF16)
        nc.vector.memset(ones[:], 1.0)
        gain_rows = consts.tile([P, 2 * HD], BF16)
        nc.vector.memset(gain_rows[:], 0.0)
        nc.scalar.dma_start(out=gain_rows[0:1, 0:HD], in_=q_scale.rearrange("(o d) -> o d", o=1))
        nc.scalar.dma_start(
            out=gain_rows[0:1, HD : 2 * HD], in_=k_scale.rearrange("(o d) -> o d", o=1)
        )
        warm = consts.tile([P, 1], F32)
        nc.scalar.activation(out=warm[:], in_=eps[:], func=ACT.Abs_reciprocal_sqrt)
        ident = consts.tile([P, P], F32)
        make_identity(nc, ident[:])

        w_grouped = consts.tile([P, N_OUT, PACK], BF16, align_bytes=64)
        nc.vector.tensor_copy(
            out=w_grouped[:, 0 : 2 * HD, :], in_=w_raws[0][:].rearrange("p t c -> p c t")
        )
        nc.scalar.copy(
            out=w_grouped[:, 2 * HD : 3 * HD, :], in_=w_raws[1][:].rearrange("p t c -> p c t")
        )
        nc.scalar.copy(
            out=w_grouped[:, 3 * HD : 4 * HD, :], in_=w_raws[2][:].rearrange("p t c -> p c t")
        )
        w_codes = consts.tile([P, N_OUT], U32, align_bytes=64)
        w_scales = consts.tile([P, N_OUT], U8, align_bytes=64)
        nc.vector.quantize_mx(
            out=w_codes[:].bitcast(FP8X4),
            scales=w_scales[:],
            in_=w_grouped[:].rearrange("p c t -> p (c t)"),
        )

        gain = consts.tile([P, 2 * HD], F32)

        def spread_gains():
            gain_ps = psum_acc.tile([P, N_OUT], F32, tag="acc")
            nc.tensor.matmul(
                out=gain_ps[:, 0 : 2 * HD], lhsT=ones[:], rhs=gain_rows[:], start=True, stop=True
            )
            nc.vector.tensor_scalar_add(out=gain[:], in0=gain_ps[:, 0 : 2 * HD], scalar1=1.0)

        out_views = [
            out_0.flatten_outer_dims().rearrange("(h p j) d -> h p j d", h=2, p=P)[0],
            out_0.flatten_outer_dims().rearrange("(h p j) d -> h p j d", h=2, p=P)[1],
            out_1.flatten_outer_dims().rearrange("(p j) d -> p j d", p=P),
            out_2.flatten_outer_dims().rearrange("(p j) d -> p j d", p=P),
        ]

        live = {}

        def transposes(u):
            xt = psum_xt.tile([P, UNIT, 2, P], F32)
            for i in range(UNIT):
                for half in range(2):
                    nc.tensor.transpose(
                        xt[:, i, half, :],
                        x_words[u * UNIT + i][:, half * P : (half + 1) * P],
                        ident[:],
                    )
            live["xt", u] = xt

        def copy_out(u):
            grouped = work.tile([P, UNIT * P * PACK], BF16, align_bytes=64)
            interleaved = grouped[:].bitcast(F32).rearrange("p (i n h) -> p i n h", i=UNIT, h=2)
            planes = live["xt", u][:].rearrange("p i h n -> p i n h")
            nc.scalar.copy(out=interleaved, in_=planes)
            live["grouped", u] = grouped

        def quantise(u):
            codes = work.tile([P, UNIT * P], U32, align_bytes=64)
            scales = work.tile([P, UNIT * P], U8, align_bytes=64)
            nc.vector.quantize_mx(
                out=codes[:].bitcast(FP8X4), scales=scales[:], in_=live["grouped", u][:]
            )
            live["codes", u] = (codes, scales)

        def project(u):
            codes, scales = live["codes", u]
            accs = []
            for i in range(UNIT):
                acc = psum_acc.tile([P, N_OUT], F32, tag="acc")
                nc.tensor.matmul_mx(
                    out=acc[:],
                    lhsT=codes[:, i * P : (i + 1) * P].bitcast(FP8X4),
                    lhsT_scale=scales[:, i * P : (i + 1) * P],
                    rhs=w_codes[:].bitcast(FP8X4),
                    rhs_scale=w_scales[:],
                    start=True,
                    stop=True,
                )
                accs.append(acc)
            live["accs", u] = accs

        def squares(u):
            squared = work.tile([P, UNIT * NORMED, HD], F32)
            sums = work.tile([P, UNIT * NORMED], F32)
            for i in range(UNIT):
                for h in range(NORMED):
                    c = i * NORMED + h
                    nc.scalar.activation(
                        out=squared[:, c, :],
                        in_=live["accs", u][i][:, h * HD : (h + 1) * HD],
                        func=ACT.Square,
                        accum_out=sums[:, c : c + 1],
                    )
            live["sums", u] = sums

        def inverse_rms(u):
            rstd = work.tile([P, UNIT * NORMED], F32)
            nc.scalar.activation(
                out=rstd[:],
                in_=live["sums", u][:],
                func=ACT.Abs_reciprocal_sqrt,
                scale=1.0 / HD,
                bias=eps[:],
            )
            live["rstd", u] = rstd

        def write_out(u):
            first_tile = u * UNIT
            if first_tile % STORE_TILES == 0:
                stage = stages.tile([P, HEADS, STORE_TILES, HD], F32)
                live["stage"] = stage
            stage = live["stage"]
            rstd = live["rstd", u]
            accs = live["accs", u]
            for i in range(UNIT):
                s = (first_tile + i) % STORE_TILES
                for h in range(NORMED):
                    c = i * NORMED + h
                    g = h // 2
                    nc.vector.scalar_tensor_tensor(
                        out=stage[:, h, s, :],
                        in0=accs[i][:, h * HD : (h + 1) * HD],
                        scalar=rstd[:, c : c + 1],
                        in1=gain[:, g * HD : (g + 1) * HD],
                        op0=ALU.mult,
                        op1=ALU.mult,
                    )
                nc.vector.tensor_copy(
                    out=stage[:, NORMED, s, :], in_=accs[i][:, NORMED * HD : N_OUT]
                )
            if first_tile >= TILES - STORE_TILES:
                stored = UNIT
            elif (first_tile + UNIT) % STORE_TILES == 0:
                stored = STORE_TILES
            else:
                stored = 0
            if stored > 0:
                j0 = first_tile + UNIT - stored
                s0 = j0 % STORE_TILES
                for h in range(HEADS):
                    nc.sync.dma_start(
                        out=out_views[h][:, j0 : j0 + stored, :], in_=stage[:, h, s0 : s0 + stored, :]
                    )

        for r in range(-2, UNITS + 1):
            if r == 0:
                spread_gains()
            if 0 <= r + 2 < UNITS:
                transposes(r + 2)
            if 0 <= r + 1 < UNITS:
                quantise(r + 1)
                project(r + 1)
            if 0 <= r < UNITS:
                squares(r)
            if 0 <= r + 2 < UNITS:
                copy_out(r + 2)
            if 0 <= r < UNITS:
                inverse_rms(r)
            if 0 <= r - 1 < UNITS:
                write_out(r - 1)
